import numpy as np
import ml_dtypes


def mxq(x, axis, fmt="e4m3"):
    dtype, down = {"e4m3": (ml_dtypes.float8_e4m3fn, 7), "e5m2": (ml_dtypes.float8_e5m2, 14)}[fmt]
    v = np.moveaxis(np.asarray(x, np.float32).astype(ml_dtypes.bfloat16).astype(np.float64), axis, -1)
    blocks = v.reshape(v.shape[:-1] + (-1, 32))
    amax = np.abs(blocks).max(-1, keepdims=True)
    byte = np.maximum(np.where(amax > 0, np.frexp(amax)[1] - 1 + 127, 0) - down, 1)
    scale = np.exp2(byte - 127.0)
    codes = (blocks / scale).astype(np.float32).astype(dtype).astype(np.float64)
    return np.moveaxis((codes * scale).reshape(v.shape), -1, axis)


WIDE = False


def mx_kscale(k):
    if not WIDE:
        return np.ones(k)
    levels = np.array([10, -10, 5, -5, 0])
    if k % 512:
        return np.exp2(np.random.permutation(np.resize(levels, k // 32))).repeat(32)
    a = np.empty((k // 512, 16))
    for p in range(k // 512):
        a[p, :8] = np.random.permutation(np.resize(levels, 8))
        for g in range(8):
            far = levels[np.abs(levels - a[p, g]) >= 10]
            a[p, g + 8] = far[np.random.randint(len(far))]
    return np.exp2(a.ravel()).repeat(32)


BF16 = ml_dtypes.bfloat16


def bf(x):
    return np.asarray(x, np.float32).astype(BF16)


def f64(x):
    return np.asarray(x).astype(np.float64)


B, CQ, CR, HID, H, W = 2, 4096, 2048, 2048, 32, 64
P = H * W


def setup_inputs():
    s, r, t = mx_kscale(CQ), mx_kscale(CR), mx_kscale(HID)
    return {"query_features": bf(np.random.standard_normal((B, CQ, H, W)) * s[None, :, None, None]),
            "reference_features": bf(np.random.standard_normal((B, CR, H, W)) * r[None, :, None, None]),
            "Wq": bf(np.random.standard_normal((HID, CQ)) * 0.4 / np.sqrt(CQ) * t[:, None] / s[None, :]),
            "bq": bf(np.random.standard_normal(HID) * 0.1 * t),
            "Wk": bf(np.random.standard_normal((HID, CR)) * 0.4 / np.sqrt(CR) / t[:, None] / r[None, :]),
            "bk": bf(np.random.standard_normal(HID) * 0.1 / t)}


def reference(query_features, reference_features, Wq, bq, Wk, bk):
    xq = f64(query_features).reshape(B, CQ, P)
    xr = f64(reference_features).reshape(B, CR, P)
    Q = (mxq(f64(Wq), 1, "e4m3") @ mxq(xq, 1, "e4m3")) + f64(bq)[None, :, None]
    K = (mxq(f64(Wk), 1, "e4m3") @ mxq(xr, 1, "e4m3")) + f64(bk)[None, :, None]
    attn = mxq(Q, 1, "e4m3").transpose(0, 2, 1) @ mxq(K, 1, "e4m3")
    return attn.reshape(B, H, W, P)

@@ -1,0 +1,287 @@
+from contextlib import ExitStack
+
+import concourse.mybir as mybir
+from concourse.masks import make_identity
+
+B, CQ, CR, HID, NPIX = 2, 4096, 2048, 2048, 2048
+FLOPS = 2 * B * NPIX * HID * (CQ + CR + NPIX)
+
+F32 = mybir.dt.float32
+BF16 = mybir.dt.bfloat16
+U32 = mybir.dt.uint32
+U8 = mybir.dt.uint8
+FP8X4 = mybir.dt.float8_e4m3fn_x4
+IDENT = mybir.ActivationFunctionType.Identity
+
+P = 128
+PACK = 4
+KP = P * PACK
+NT = 512
+NCH = NPIX // NT
+NG = HID // KP
+PASSES = {"q": CQ // KP, "k": CR // KP}
+
+RAW_BUFS = 4
+GRP_BUFS = 3
+STG_BUFS = 3
+C8_BUFS = 5
+OUT_BUFS = 4
+
+
+def tile_crossattentionvaluefuser_pa_l_kernel(tc, query_features, reference_features, Wq, bq, Wk, bk, out):
+    nc = tc.nc
+    feats = {
+        "q": query_features.rearrange("b c h w -> b c (h w)"),
+        "k": reference_features.rearrange("b c h w -> b c (h w)"),
+    }
+    weights = {"q": Wq, "k": Wk}
+    out_rows = out.rearrange("b h w p -> b (h w) p")
+
+    with ExitStack() as ctx:
+        ctx.enter_context(tc.manual_schedule())
+        const = ctx.enter_context(tc.tile_pool(name="const", bufs=1))
+        keep = ctx.enter_context(tc.tile_pool(name="keep", bufs=1))
+        stage = ctx.enter_context(tc.tile_pool(name="stage", bufs=2))
+        psum = ctx.enter_context(tc.psum_pool(name="psum", bufs=4))
+
+        ident = const.tile([P, P], F32, name="ident")
+        make_identity(nc, ident[:])
+        bias = {}
+        for s, vec in (("q", bq), ("k", bk)):
+            b_raw = const.tile([P, NG, PACK], BF16, name="braw" + s)
+            nc.gpsimd.dma_start(out=b_raw[:], in_=vec.rearrange("(g p t) -> p g t", g=NG, t=PACK))
+            bias[s] = const.tile([P, NG * PACK], F32, name="bias" + s)
+            nc.vector.tensor_copy(out=bias[s][:], in_=b_raw[:].rearrange("p g t -> p (g t)"))
+        warm = const.tile([P, 1], F32, name="warm")
+        nc.scalar.activation(out=warm[:], in_=ident[:, 0:1], func=IDENT, bias=0.0, scale=1.0)
+
+        w_codes, w_planes = {}, {}
+        for s in ("q", "k"):
+            for G in range(NG):
+                w_codes[s, G] = keep.tile([P, PASSES[s], KP], U32, name="wc%s%d" % (s, G), align_bytes=64)
+                w_planes[s, G] = keep.tile([P, PASSES[s] // 4, KP], U8, name="wp%s%d" % (s, G), align_bytes=64)
+
+        load_list = []
+        load_pos = {}
+        raws = {}
+        issued = [0]
+
+        def view_of(key):
+            if key[0] == "w":
+                s, G, g = key[1:]
+                return weights[s][KP * G : KP * (G + 1), KP * g : KP * (g + 1)].rearrange("(m t) k -> m t k", t=PACK)
+            s, b, n, g = key[1:]
+            return feats[s][b, KP * g : KP * (g + 1), NT * n : NT * (n + 1)].rearrange("(p j) w -> p j w", j=PACK)
+
+        def fetch(key):
+            want = min(len(load_list), load_pos[key] + RAW_BUFS)
+            while issued[0] < want:
+                k2 = load_list[issued[0]]
+                raw = stage.tile([P, PACK, NT], BF16, name="raw", bufs=RAW_BUFS)
+                nc.sync.dma_start(out=raw[:], in_=view_of(k2))
+                raws[k2] = raw
+                issued[0] += 1
+            return raws[key]
+
+        def interleave(engine, src):
+            grp = stage.tile([P, NT * PACK], BF16, name="grp", bufs=GRP_BUFS, align_bytes=64)
+            dst = grp[:].rearrange("p (w j) -> p w j", j=PACK)
+            if engine == "v":
+                nc.vector.tensor_copy(out=dst, in_=src[:].rearrange("p j w -> p w j"))
+            else:
+                nc.scalar.copy(out=dst, in_=src[:].rearrange("p j w -> p w j"))
+            return grp
+
+        def quantize(grp, codes, plane, slot):
+            nc.vector.quantize_mx(out=codes.bitcast(FP8X4), scales=plane[4 * slot : P, :], in_=grp[:])
+
+        def new_c8():
+            codes = stage.tile([P, 4, NT], U32, name="c8", bufs=C8_BUFS, align_bytes=64)
+            plane = stage.tile([P, NT], U8, name="c8p", bufs=C8_BUFS, align_bytes=64)
+            return codes, plane
+
+        def w_transpose(units):
+            banks = []
+            for s, G, g in units:
+                words = fetch(("w", s, G, g))[:].rearrange("m t k -> m (t k)").bitcast(F32)
+                for half in range(2):
+                    bank = psum.tile([P, NT], F32, name="pb")
+                    for tt in range(2):
+                        t = 2 * half + tt
+                        for u in range(2):
+                            c0 = (2 * tt + u) * P
+                            nc.tensor.transpose(bank[:, c0 : c0 + P], words[:, 256 * t + u : 256 * (t + 1) : 2], ident[:])
+                    banks.append(bank)
+            return banks
+
+        def w_finish_s(units, banks):
+            tiles = []
+            for i in range(len(units)):
+                wg = stage.tile([P, NT * PACK], BF16, name="stg", bufs=STG_BUFS, align_bytes=64)
+                wgw = wg[:].bitcast(F32)
+                for half in range(2):
+                    nc.scalar.copy(
+                        out=wgw[:, 512 * half : 512 * (half + 1)].rearrange("p (t m u) -> p t m u", t=2, u=2),
+                        in_=banks[2 * i + half][:].rearrange("p (t u m) -> p t m u", t=2, u=2),
+                    )
+                tiles.append(wg)
+            return tiles
+
+        def w_finish_v(units, tiles):
+            for (s, G, g), wg in zip(units, tiles):
+                quantize(wg, w_codes[s, G][:, g, :], w_planes[s, G][:, g // 4, :], g % 4)
+
+        def s1_matmul(acc, s, G, t, g, xc):
+            codes, plane = xc[g // 4]
+            nc.tensor.matmul_mx(
+                out=acc[:],
+                lhsT=w_codes[s, G][:, g, P * t : P * (t + 1)].bitcast(FP8X4),
+                lhsT_scale=w_planes[s, G][4 * (g % 4) : P, g // 4, P * t : P * (t + 1)],
+                rhs=codes[:, g % 4, :].bitcast(FP8X4),
+                rhs_scale=plane[4 * (g % 4) : P, :],
+                start=(g == 0),
+                stop=(g == PASSES[s] - 1),
+            )
+
+        def s1_evacuate(accs, s, G):
+            st = stage.tile([P, PACK, NT], BF16, name="stg", bufs=STG_BUFS, align_bytes=64)
+            for t in range(PACK):
+                col = PACK * G + t
+                nc.scalar.activation(out=st[:, t, :], in_=accs[t][:], func=IDENT, bias=bias[s][:, col : col + 1], scale=1.0)
+            return st
+
+        def s2_part(b, n, part, q_tiles, kc):
+            for it in range(4 * part, 4 * part + 4):
+                qc, qp = q_tiles[it // 4]
+                c0 = (it % 4) * P
+                acc = psum.tile([P, NT], F32, name="pb")
+                for G in range(NG):
+                    nc.tensor.matmul_mx(
+                        out=acc[:],
+                        lhsT=qc[:, G, c0 : c0 + P].bitcast(FP8X4),
+                        lhsT_scale=qp[4 * G : P, c0 : c0 + P],
+                        rhs=kc[0][:, G, :].bitcast(FP8X4),
+                        rhs_scale=kc[1][4 * G : P, :],
+                        start=(G == 0),
+                        stop=(G == NG - 1),
+                    )
+                o = stage.tile([P, NT], F32, name="o", bufs=OUT_BUFS)
+                nc.scalar.copy(out=o[:], in_=acc[:])
+                nc.scalar.dma_start(out=out_rows[b, P * it : P * (it + 1), NT * n : NT * (n + 1)], in_=o[:])
+
+        wq_units = [("q", u // 8, u % 8) for u in range(32)]
+        wk_units = [("k", u // 4, u % 4) for u in range(16)]
+        blocks = [dict(T=wq_units[0:2], nx=2)]
+        for j in range(16):
+            blocks.append(dict(T=wq_units[2 * j + 2 : 2 * j + 4], TM=j, nx=(2 if j < 3 else (1 if 4 <= j < 12 else 0))))
+        for b in range(B):
+            for n in range(NCH):
+                if b == 0 and n == 0:
+                    continue
+                for G in range(NG):
+                    blk = dict(T=[], S1=("q", b, n, G), nx=(2 if n < NCH - 1 else 1))
+                    if b == 0 and n <= 2:
+                        i = 4 * (n - 1) + G
+                        blk["T"] = wk_units[2 * i : 2 * i + 2]
+                    if b == 1 and n == 0:
+                        blk["S2"] = (0, NCH - 1, G)
+                    blocks.append(blk)
+            for n in range(NCH):
+                for G in range(NG):
+                    blk = dict(T=[], S1=("k", b, n, G), nx=1)
+                    if n > 0:
+                        blk["S2"] = (b, n - 1, G)
+                    if n == NCH - 1:
+                        blk["nx"] = 2 if b == 0 else 0
+                    blocks.append(blk)
+        for G in range(NG):
+            blocks.append(dict(T=[], S2=(B - 1, NCH - 1, G), nx=0))
+
+        x_list = []
+        for b in range(B):
+            for s in ("q", "k"):
+                for n in range(NCH):
+                    for g in range(PASSES[s]):
+                        x_list.append((s, b, n, g))
+        x_next = [0]
+
+        xi = 0
+        for blk in blocks:
+            for unit in blk["T"]:
+                load_list.append(("w",) + unit)
+            for i in range(blk["nx"]):
+                load_list.append(("x",) + x_list[xi])
+                xi += 1
+        assert xi == len(x_list)
+        for i, key in enumerate(load_list):
+            load_pos[key] = i
+
+        x_codes = {}
+        q_tiles = {}
+        k_tiles = {}
+        accs = {}
+        pending = []
+
+        for bi, blk in enumerate(blocks):
+            head = bi < 4
+            banks = w_transpose(blk["T"]) if blk["T"] else []
+
+            todo = []
+            for st, codes, plane, slot in pending:
+                todo.append((interleave("v", st), codes, plane, slot))
+            pending = []
+            for i in range(blk["nx"]):
+                s, b, n, g = x_list[x_next[0]]
+                x_next[0] += 1
+                if g % 4 == 0:
+                    if g == 0:
+                        x_codes[s, b, n] = []
+                    x_codes[s, b, n].append(new_c8())
+                codes, plane = x_codes[s, b, n][g // 4]
+                raw = fetch(("x", s, b, n, g))
+                todo.append((interleave("s" if (head and i == 1) else "v", raw), codes[:, g % 4, :], plane, g % 4))
+            for grp, codes, plane, slot in todo:
+                quantize(grp, codes, plane, slot)
+
+            if "TM" in blk:
+                j = blk["TM"]
+                G = j // 4
+                for g in (2 * j % 8, 2 * j % 8 + 1):
+                    if g == 0:
+                        for t in range(PACK):
+                            accs[t] = psum.tile([P, NT], F32, name="pa")
+                    for t in range(PACK):
+                        s1_matmul(accs[t], "q", G, t, g, x_codes["q", 0, 0])
+            s1 = blk.get("S1")
+            if s1 is not None:
+                s, b, n, G = s1
+                for t in range(PACK):
+                    accs[t] = psum.tile([P, NT], F32, name="pa")
+                    for g in range(PASSES[s]):
+                        s1_matmul(accs[t], s, G, t, g, x_codes[s, b, n])
+
+            if banks:
+                w_finish_v(blk["T"], w_finish_s(blk["T"], banks))
+
+            if "TM" in blk and blk["TM"] % 4 == 3:
+                s1 = ("q", 0, 0, blk["TM"] // 4)
+            if s1 is not None:
+                s, b, n, G = s1
+                st = s1_evacuate(accs, s, G)
+                if s == "q":
+                    if G == 0:
+                        if n == 0:
+                            q_tiles[b] = []
+                        qc = keep.tile([P, NG, NT], U32, name="qc%d" % n, align_bytes=64)
+                        qp = keep.tile([P, NT], U8, name="qp%d" % n, align_bytes=64)
+                        q_tiles[b].append((qc, qp))
+                    dest = q_tiles[b][n]
+                else:
+                    if G == 0:
+                        k_tiles[b, n] = new_c8()
+                    dest = k_tiles[b, n]
+                pending.append((st, dest[0][:, G, :], dest[1], G))
+
+            if "S2" in blk:
+                b, n, part = blk["S2"]
+                s2_part(b, n, part, q_tiles[b], k_tiles[b, n])

@@ -23,9 +23,50 @@ PASSES = {"q": CQ // KP, "k": CR // KP}
 
 RAW_BUFS = 4
 GRP_BUFS = 3
-STG_BUFS = 3
+STG_BUFS = 4
 C8_BUFS = 5
 OUT_BUFS = 4
+BORROW = ("wck0", "wck1", "wck2", "wck3", "qc1", "qc2", "qc3")
+HEAD_TILES = 8
+HEAD_SCALAR_COLS = 192
+SORT_Q_FROM = 4
+
+
+def is_sorted(unit):
+    return unit[0] == "k" or unit[1] >= SORT_Q_FROM
+
+
+def plan():
+    wq = [("q", u // 8, u % 8) for u in range(32)]
+    wk = [("k", u // 4, u % 4) for u in range(16)]
+    blocks = [dict(T=wq[0:1], nx=1), dict(T=wq[1:2], nx=1)]
+    for g in range(8):
+        blocks.append(dict(T=wq[g + 2 : g + 3], M=wq[g : g + 1], nx=(1 if g < 6 else 0)))
+    for j in range(4, 16):
+        blocks.append(dict(T=wq[2 * j + 2 : 2 * j + 4], M=wq[2 * j : 2 * j + 2], nx=(1 if j < 12 else 0)))
+    for b in range(B):
+        for n in range(NCH):
+            if b == 0 and n == 0:
+                continue
+            for G in range(NG):
+                blk = dict(T=[], S1=("q", b, n, G), nx=(2 if n < NCH - 1 else 1))
+                if b == 0 and n <= 2:
+                    i = 4 * (n - 1) + G
+                    blk["T"] = wk[2 * i : 2 * i + 2]
+                if b == 1 and n == 0:
+                    blk["S2"] = (0, NCH - 1, G)
+                blocks.append(blk)
+        for n in range(NCH):
+            for G in range(NG):
+                blk = dict(T=[], S1=("k", b, n, G), nx=1)
+                if n > 0:
+                    blk["S2"] = (b, n - 1, G)
+                if n == NCH - 1:
+                    blk["nx"] = 2 if b == 0 else 0
+                blocks.append(blk)
+    for G in range(NG):
+        blocks.append(dict(T=[], S2=(B - 1, NCH - 1, G), nx=0))
+    return blocks
 
 
 def tile_crossattentionvaluefuser_pa_l_kernel(tc, query_features, reference_features, Wq, bq, Wk, bk, out):
@@ -44,27 +85,34 @@ def tile_crossattentionvaluefuser_pa_l_kernel(tc, query_features, reference_feat
         stage = ctx.enter_context(tc.tile_pool(name="stage", bufs=2))
         psum = ctx.enter_context(tc.psum_pool(name="psum", bufs=4))
 
-        ident = const.tile([P, P], F32, name="ident")
-        make_identity(nc, ident[:])
-        bias = {}
-        for s, vec in (("q", bq), ("k", bk)):
-            b_raw = const.tile([P, NG, PACK], BF16, name="braw" + s)
-            nc.gpsimd.dma_start(out=b_raw[:], in_=vec.rearrange("(g p t) -> p g t", g=NG, t=PACK))
-            bias[s] = const.tile([P, NG * PACK], F32, name="bias" + s)
-            nc.vector.tensor_copy(out=bias[s][:], in_=b_raw[:].rearrange("p g t -> p (g t)"))
-        warm = const.tile([P, 1], F32, name="warm")
-        nc.scalar.activation(out=warm[:], in_=ident[:, 0:1], func=IDENT, bias=0.0, scale=1.0)
-
-        w_codes, w_planes = {}, {}
-        for s in ("q", "k"):
-            for G in range(NG):
-                w_codes[s, G] = keep.tile([P, PASSES[s], KP], U32, name="wc%s%d" % (s, G), align_bytes=64)
-                w_planes[s, G] = keep.tile([P, PASSES[s] // 4, KP], U8, name="wp%s%d" % (s, G), align_bytes=64)
+        blocks = plan()
+        x_list = []
+        for b in range(B):
+            for s in ("q", "k"):
+                for n in range(NCH):
+                    for g in range(PASSES[s]):
+                        x_list.append((s, b, n, g))
 
         load_list = []
+        xi = 0
+        for i, blk in enumerate(blocks):
+            for unit in blk["T"]:
+                if not is_sorted(unit):
+                    load_list.append(("w",) + unit)
+            for r in range(blk["nx"]):
+                load_list.append(("x",) + x_list[xi])
+                xi += 1
+            if i + 1 < len(blocks):
+                for unit in blocks[i + 1]["T"]:
+                    if is_sorted(unit):
+                        load_list.append(("w",) + unit)
+        assert xi == len(x_list)
         load_pos = {}
+        for i, key in enumerate(load_list):
+            load_pos[key] = i
         raws = {}
         issued = [0]
+        lent = [None]
 
         def view_of(key):
             if key[0] == "w":
@@ -74,22 +122,44 @@ def tile_crossattentionvaluefuser_pa_l_kernel(tc, query_features, reference_feat
             return feats[s][b, KP * g : KP * (g + 1), NT * n : NT * (n + 1)].rearrange("(p j) w -> p j w", j=PACK)
 
         def fetch(key):
-            want = min(len(load_list), load_pos[key] + RAW_BUFS)
+            want = min(len(load_list), max(load_pos[key], 2 * len(BORROW)) + RAW_BUFS)
             while issued[0] < want:
-                k2 = load_list[issued[0]]
-                raw = stage.tile([P, PACK, NT], BF16, name="raw", bufs=RAW_BUFS)
+                i = issued[0]
+                k2 = load_list[i]
+                if i < 2 * len(BORROW):
+                    if i % 2 == 0:
+                        lent[0] = keep.tile([P, 2, PACK, NT], BF16, name=BORROW[i // 2], align_bytes=64)
+                    raw = lent[0][:, i % 2]
+                else:
+                    raw = stage.tile([P, PACK, NT], BF16, name="raw", bufs=RAW_BUFS)
                 nc.sync.dma_start(out=raw[:], in_=view_of(k2))
                 raws[k2] = raw
                 issued[0] += 1
             return raws[key]
 
-        def interleave(engine, src):
+        fetch(load_list[0])
+
+        ident = const.tile([P, P], F32, name="ident")
+        make_identity(nc, ident[:])
+        bias = {}
+        bias_raw = {}
+        for s, vec in (("q", bq), ("k", bk)):
+            b_raw = const.tile([P, NG, PACK], BF16, name="braw" + s)
+            nc.gpsimd.dma_start(out=b_raw[:], in_=vec.rearrange("(g p t) -> p g t", g=NG, t=PACK))
+            bias[s] = const.tile([P, NG * PACK], F32, name="bias" + s)
+            bias_raw[s] = b_raw
+        warm = const.tile([P, 1], F32, name="warm")
+        nc.scalar.activation(out=warm[:], in_=ident[:, 0:1], func=IDENT, bias=0.0, scale=1.0)
+
+        w_codes, w_planes = {}, {}
+
+        def interleave(src, scalar_cols):
             grp = stage.tile([P, NT * PACK], BF16, name="grp", bufs=GRP_BUFS, align_bytes=64)
             dst = grp[:].rearrange("p (w j) -> p w j", j=PACK)
-            if engine == "v":
-                nc.vector.tensor_copy(out=dst, in_=src[:].rearrange("p j w -> p w j"))
-            else:
-                nc.scalar.copy(out=dst, in_=src[:].rearrange("p j w -> p w j"))
+            cut = NT - scalar_cols
+            nc.vector.tensor_copy(out=dst[:, 0:cut, :], in_=src[:, :, 0:cut].rearrange("p j w -> p w j"))
+            if scalar_cols:
+                nc.scalar.copy(out=dst[:, cut:NT, :], in_=src[:, :, cut:NT].rearrange("p j w -> p w j"))
             return grp
 
         def quantize(grp, codes, plane, slot):
@@ -100,21 +170,43 @@ def tile_crossattentionvaluefuser_pa_l_kernel(tc, query_features, reference_feat
             plane = stage.tile([P, NT], U8, name="c8p", bufs=C8_BUFS, align_bytes=64)
             return codes, plane
 
+        sorted_words = {}
+
+        def w_sort(unit):
+            words = fetch(("w",) + unit)[:].rearrange("m t k -> m (t k)").bitcast(F32)
+            srt = stage.tile([P, 2 * NT], F32, name="stg", bufs=STG_BUFS, align_bytes=64)
+            nc.scalar.copy(
+                out=srt[:].rearrange("m (t u p) -> m t u p", t=PACK, u=2),
+                in_=words.rearrange("m (t p u) -> m t u p", t=PACK, u=2),
+            )
+            sorted_words[unit] = srt
+
         def w_transpose(units):
             banks = []
-            for s, G, g in units:
-                words = fetch(("w", s, G, g))[:].rearrange("m t k -> m (t k)").bitcast(F32)
+            for unit in units:
+                s, G, g = unit
+                if g == 0:
+                    w_codes[s, G] = keep.tile([P, PASSES[s], KP], U32, name="wc%s%d" % (s, G), align_bytes=64)
+                    w_planes[s, G] = keep.tile([P, PASSES[s] // 4, KP], U8, name="wp%s%d" % (s, G), align_bytes=64)
+                if is_sorted(unit):
+                    words = sorted_words[unit]
+                else:
+                    words = fetch(("w",) + unit)[:].rearrange("m t k -> m (t k)").bitcast(F32)
                 for half in range(2):
                     bank = psum.tile([P, NT], F32, name="pb")
                     for tt in range(2):
                         t = 2 * half + tt
                         for u in range(2):
                             c0 = (2 * tt + u) * P
-                            nc.tensor.transpose(bank[:, c0 : c0 + P], words[:, 256 * t + u : 256 * (t + 1) : 2], ident[:])
+                            if is_sorted(unit):
+                                src = words[:, (2 * t + u) * P : (2 * t + u + 1) * P]
+                            else:
+                                src = words[:, 256 * t + u : 256 * (t + 1) : 2]
+                            nc.tensor.transpose(bank[:, c0 : c0 + P], src, ident[:])
                     banks.append(bank)
             return banks
 
-        def w_finish_s(units, banks):
+        def w_evacuate(units, banks):
             tiles = []
             for i in range(len(units)):
                 wg = stage.tile([P, NT * PACK], BF16, name="stg", bufs=STG_BUFS, align_bytes=64)
@@ -126,10 +218,6 @@ def tile_crossattentionvaluefuser_pa_l_kernel(tc, query_features, reference_feat
                     )
                 tiles.append(wg)
             return tiles
-
-        def w_finish_v(units, tiles):
-            for (s, G, g), wg in zip(units, tiles):
-                quantize(wg, w_codes[s, G][:, g, :], w_planes[s, G][:, g // 4, :], g % 4)
 
         def s1_matmul(acc, s, G, t, g, xc):
             codes, plane = xc[g // 4]
@@ -169,102 +257,73 @@ def tile_crossattentionvaluefuser_pa_l_kernel(tc, query_features, reference_feat
                 nc.scalar.copy(out=o[:], in_=acc[:])
                 nc.scalar.dma_start(out=out_rows[b, P * it : P * (it + 1), NT * n : NT * (n + 1)], in_=o[:])
 
-        wq_units = [("q", u // 8, u % 8) for u in range(32)]
-        wk_units = [("k", u // 4, u % 4) for u in range(16)]
-        blocks = [dict(T=wq_units[0:2], nx=2)]
-        for j in range(16):
-            blocks.append(dict(T=wq_units[2 * j + 2 : 2 * j + 4], TM=j, nx=(2 if j < 3 else (1 if 4 <= j < 12 else 0))))
-        for b in range(B):
-            for n in range(NCH):
-                if b == 0 and n == 0:
-                    continue
-                for G in range(NG):
-                    blk = dict(T=[], S1=("q", b, n, G), nx=(2 if n < NCH - 1 else 1))
-                    if b == 0 and n <= 2:
-                        i = 4 * (n - 1) + G
-                        blk["T"] = wk_units[2 * i : 2 * i + 2]
-                    if b == 1 and n == 0:
-                        blk["S2"] = (0, NCH - 1, G)
-                    blocks.append(blk)
-            for n in range(NCH):
-                for G in range(NG):
-                    blk = dict(T=[], S1=("k", b, n, G), nx=1)
-                    if n > 0:
-                        blk["S2"] = (b, n - 1, G)
-                    if n == NCH - 1:
-                        blk["nx"] = 2 if b == 0 else 0
-                    blocks.append(blk)
-        for G in range(NG):
-            blocks.append(dict(T=[], S2=(B - 1, NCH - 1, G), nx=0))
-
-        x_list = []
-        for b in range(B):
-            for s in ("q", "k"):
-                for n in range(NCH):
-                    for g in range(PASSES[s]):
-                        x_list.append((s, b, n, g))
-        x_next = [0]
-
-        xi = 0
-        for blk in blocks:
-            for unit in blk["T"]:
-                load_list.append(("w",) + unit)
-            for i in range(blk["nx"]):
-                load_list.append(("x",) + x_list[xi])
-                xi += 1
-        assert xi == len(x_list)
-        for i, key in enumerate(load_list):
-            load_pos[key] = i
-
         x_codes = {}
         q_tiles = {}
         k_tiles = {}
         accs = {}
         pending = []
+        x_next = 0
+        late_x = {}
+        w_ready = {}
 
         for bi, blk in enumerate(blocks):
-            head = bi < 4
-            banks = w_transpose(blk["T"]) if blk["T"] else []
+            if bi == 4:
+                for s in ("q", "k"):
+                    nc.vector.tensor_copy(out=bias[s][:], in_=bias_raw[s][:].rearrange("p g t -> p (g t)"))
+            units = blk["T"]
+            banks = w_transpose(units)
 
             todo = []
             for st, codes, plane, slot in pending:
-                todo.append((interleave("v", st), codes, plane, slot))
+                todo.append((interleave(st, 0), codes, plane, slot))
             pending = []
-            for i in range(blk["nx"]):
-                s, b, n, g = x_list[x_next[0]]
-                x_next[0] += 1
+            for r in range(blk["nx"]):
+                s, b, n, g = x_list[x_next]
                 if g % 4 == 0:
                     if g == 0:
                         x_codes[s, b, n] = []
                     x_codes[s, b, n].append(new_c8())
                 codes, plane = x_codes[s, b, n][g // 4]
                 raw = fetch(("x", s, b, n, g))
-                todo.append((interleave("s" if (head and i == 1) else "v", raw), codes[:, g % 4, :], plane, g % 4))
+                if x_next < HEAD_TILES:
+                    late_x[g] = (interleave(raw, HEAD_SCALAR_COLS), codes[:, g % 4, :], plane, g % 4)
+                else:
+                    todo.append((interleave(raw, 0), codes[:, g % 4, :], plane, g % 4))
+                x_next += 1
             for grp, codes, plane, slot in todo:
                 quantize(grp, codes, plane, slot)
+            for unit, wg in zip(units, w_evacuate(units, banks)):
+                w_ready[unit] = wg
 
-            if "TM" in blk:
-                j = blk["TM"]
-                G = j // 4
-                for g in (2 * j % 8, 2 * j % 8 + 1):
-                    if g == 0:
-                        for t in range(PACK):
-                            accs[t] = psum.tile([P, NT], F32, name="pa")
-                    for t in range(PACK):
-                        s1_matmul(accs[t], "q", G, t, g, x_codes["q", 0, 0])
             s1 = blk.get("S1")
-            if s1 is not None:
+            for s, G, g in blk.get("M", []):
+                if g == 0:
+                    for t in range(PACK):
+                        accs[t] = psum.tile([P, NT], F32, name="pa")
+                for t in range(PACK):
+                    s1_matmul(accs[t], s, G, t, g, x_codes[s, 0, 0])
+                if g == PASSES[s] - 1:
+                    s1 = (s, 0, 0, G)
+            if "S1" in blk:
                 s, b, n, G = s1
                 for t in range(PACK):
                     accs[t] = psum.tile([P, NT], F32, name="pa")
                     for g in range(PASSES[s]):
                         s1_matmul(accs[t], s, G, t, g, x_codes[s, b, n])
 
-            if banks:
-                w_finish_v(blk["T"], w_finish_s(blk["T"], banks))
+            due = [u for u in units if u[0] == "k"]
+            if bi + 1 < len(blocks):
+                due = due + blocks[bi + 1].get("M", [])
+            for s, G, g in due:
+                quantize(w_ready[s, G, g], w_codes[s, G][:, g, :], w_planes[s, G][:, g // 4, :], g % 4)
+                if s == "q" and G == 0:
+                    quantize(*late_x[g])
 
-            if "TM" in blk and blk["TM"] % 4 == 3:
-                s1 = ("q", 0, 0, blk["TM"] // 4)
+            if bi + 1 < len(blocks):
+                for unit in blocks[bi + 1]["T"]:
+                    if is_sorted(unit):
+                        w_sort(unit)
+
             if s1 is not None:
                 s, b, n, G = s1
                 st = s1_evacuate(accs, s, G)

@@ -27,6 +27,7 @@ STG_BUFS = 4
 C8_BUFS = 5
 OUT_BUFS = 4
 BORROW = ("wck0", "wck1", "wck2", "wck3", "qc1", "qc2", "qc3")
+SHIFT = 64
 HEAD_TILES = 8
 HEAD_SCALAR_COLS = 192
 SORT_Q_FROM = 4
@@ -128,7 +129,7 @@ def tile_crossattentionvaluefuser_pa_l_kernel(tc, query_features, reference_feat
                 k2 = load_list[i]
                 if i < 2 * len(BORROW):
                     if i % 2 == 0:
-                        lent[0] = keep.tile([P, 2, PACK, NT], BF16, name=BORROW[i // 2], align_bytes=64)
+                        lent[0] = keep.tile([P, 2, PACK, NT], BF16, name=BORROW[i // 2], align_bytes=256)
                     raw = lent[0][:, i % 2]
                 else:
                     raw = stage.tile([P, PACK, NT], BF16, name="raw", bufs=RAW_BUFS)
@@ -152,6 +153,7 @@ def tile_crossattentionvaluefuser_pa_l_kernel(tc, query_features, reference_feat
         nc.scalar.activation(out=warm[:], in_=ident[:, 0:1], func=IDENT, bias=0.0, scale=1.0)
 
         w_codes, w_planes = {}, {}
+        w_plane_tile = {}
 
         def interleave(src, scalar_cols):
             grp = stage.tile([P, NT * PACK], BF16, name="grp", bufs=GRP_BUFS, align_bytes=64)
@@ -166,9 +168,9 @@ def tile_crossattentionvaluefuser_pa_l_kernel(tc, query_features, reference_feat
             nc.vector.quantize_mx(out=codes.bitcast(FP8X4), scales=plane[4 * slot : P, :], in_=grp[:])
 
         def new_c8():
-            codes = stage.tile([P, 4, NT], U32, name="c8", bufs=C8_BUFS, align_bytes=64)
-            plane = stage.tile([P, NT], U8, name="c8p", bufs=C8_BUFS, align_bytes=64)
-            return codes, plane
+            codes = stage.tile([P, 4, NT], U32, name="c8", bufs=C8_BUFS, align_bytes=256)
+            plane = stage.tile([P, NT + SHIFT], U8, name="c8p", bufs=C8_BUFS, align_bytes=256)
+            return codes, plane[:, SHIFT : SHIFT + NT]
 
         sorted_words = {}
 
@@ -186,8 +188,11 @@ def tile_crossattentionvaluefuser_pa_l_kernel(tc, query_features, reference_feat
             for unit in units:
                 s, G, g = unit
                 if g == 0:
-                    w_codes[s, G] = keep.tile([P, PASSES[s], KP], U32, name="wc%s%d" % (s, G), align_bytes=64)
-                    w_planes[s, G] = keep.tile([P, PASSES[s] // 4, KP], U8, name="wp%s%d" % (s, G), align_bytes=64)
+                    w_codes[s, G] = keep.tile([P, PASSES[s], KP], U32, name="wc%s%d" % (s, G), align_bytes=256)
+                    width = PASSES[s] // 4 * KP
+                    if G == 0:
+                        w_plane_tile[s] = keep.tile([P, NG * width + SHIFT], U8, name="wp%s" % s, align_bytes=256)
+                    w_planes[s, G] = w_plane_tile[s][:, SHIFT + G * width : SHIFT + (G + 1) * width].rearrange("p (h c) -> p h c", c=KP)
                 if is_sorted(unit):
                     words = sorted_words[unit]
                 else:
@@ -331,9 +336,9 @@ def tile_crossattentionvaluefuser_pa_l_kernel(tc, query_features, reference_feat
                     if G == 0:
                         if n == 0:
                             q_tiles[b] = []
-                        qc = keep.tile([P, NG, NT], U32, name="qc%d" % n, align_bytes=64)
-                        qp = keep.tile([P, NT], U8, name="qp%d" % n, align_bytes=64)
-                        q_tiles[b].append((qc, qp))
+                        qc = keep.tile([P, NG, NT], U32, name="qc%d" % n, align_bytes=256)
+                        qp = keep.tile([P, NT + SHIFT], U8, name="qp%d" % n, align_bytes=256)
+                        q_tiles[b].append((qc, qp[:, SHIFT : SHIFT + NT]))
                     dest = q_tiles[b][n]
                 else:
                     if G == 0:

@@ -243,14 +243,21 @@ def tile_crossattentionvaluefuser_pa_l_kernel(tc, query_features, reference_feat
                 nc.scalar.activation(out=st[:, t, :], in_=accs[t][:], func=IDENT, bias=bias[s][:, col : col + 1], scale=1.0)
             return st
 
-        def s2_part(b, n, part, q_tiles, kc):
-            for it in range(4 * part, 4 * part + 4):
-                qc, qp = q_tiles[it // 4]
-                c0 = (it % 4) * P
-                acc = psum.tile([P, NT], F32, name="pb")
-                for G in range(NG):
+        def s2_part(b, n, part, q_tiles, kc, tag):
+            qc, qp = q_tiles[part]
+            banks4 = []
+            for i4 in range(4):
+                acc4 = psum.tile([P, NT], F32, name=tag)
+                banks4.append(acc4)
+            if b == B - 1 and n == NCH - 1 and part == 3:
+                order = [(G, i4) for i4 in range(4) for G in range(NG)]
+            else:
+                order = [(G, i4) for G in range(NG) for i4 in range(4)]
+            for G, i4 in order:
+                if True:
+                    c0 = i4 * P
                     nc.tensor.matmul_mx(
-                        out=acc[:],
+                        out=banks4[i4][:],
                         lhsT=qc[:, G, c0 : c0 + P].bitcast(FP8X4),
                         lhsT_scale=qp[4 * G : P, c0 : c0 + P],
                         rhs=kc[0][:, G, :].bitcast(FP8X4),
@@ -258,8 +265,10 @@ def tile_crossattentionvaluefuser_pa_l_kernel(tc, query_features, reference_feat
                         start=(G == 0),
                         stop=(G == NG - 1),
                     )
+            for i4 in range(4):
+                it = 4 * part + i4
                 o = stage.tile([P, NT], F32, name="o", bufs=OUT_BUFS)
-                nc.scalar.copy(out=o[:], in_=acc[:])
+                nc.scalar.copy(out=o[:], in_=banks4[i4][:])
                 nc.scalar.dma_start(out=out_rows[b, P * it : P * (it + 1), NT * n : NT * (n + 1)], in_=o[:])
 
         x_codes = {}
@@ -268,6 +277,7 @@ def tile_crossattentionvaluefuser_pa_l_kernel(tc, query_features, reference_feat
         accs = {}
         pending = []
         x_next = 0
+        last_tag = ["pa"]
         late_x = {}
         w_ready = {}
 
@@ -311,9 +321,14 @@ def tile_crossattentionvaluefuser_pa_l_kernel(tc, query_features, reference_feat
                     s1 = (s, 0, 0, G)
             if "S1" in blk:
                 s, b, n, G = s1
+                if units or "S2" in blk or last_tag[0] == "pb":
+                    last_tag[0] = "pa"
+                else:
+                    last_tag[0] = "pb"
                 for t in range(PACK):
-                    accs[t] = psum.tile([P, NT], F32, name="pa")
-                    for g in range(PASSES[s]):
+                    accs[t] = psum.tile([P, NT], F32, name=last_tag[0])
+                for g in range(PASSES[s]):
+                    for t in range(PACK):
                         s1_matmul(accs[t], s, G, t, g, x_codes[s, b, n])
 
             due = [u for u in units if u[0] == "k"]
@@ -348,4 +363,4 @@ def tile_crossattentionvaluefuser_pa_l_kernel(tc, query_features, reference_feat
 
             if "S2" in blk:
                 b, n, part = blk["S2"]
-                s2_part(b, n, part, q_tiles[b], k_tiles[b, n])
+                s2_part(b, n, part, q_tiles[b], k_tiles[b, n], "pb" if ("S1" in blk or part % 2 == 1) else "pa")

from contextlib import ExitStack

import concourse.mybir as mybir
from concourse.masks import make_identity

B, CQ, CR, HID, NPIX = 2, 4096, 2048, 2048, 2048
FLOPS = 2 * B * NPIX * HID * (CQ + CR + NPIX)

F32 = mybir.dt.float32
BF16 = mybir.dt.bfloat16
U32 = mybir.dt.uint32
U8 = mybir.dt.uint8
FP8X4 = mybir.dt.float8_e4m3fn_x4
IDENT = mybir.ActivationFunctionType.Identity

P = 128
PACK = 4
KP = P * PACK
NT = 512
NCH = NPIX // NT
NG = HID // KP
PASSES = {"q": CQ // KP, "k": CR // KP}

RAW_BUFS = 4
GRP_BUFS = 3
STG_BUFS = 4
C8_BUFS = 5
OUT_BUFS = 4
BORROW = ("wck0", "wck1", "wck2", "wck3", "qc1", "qc2", "qc3")
SHIFT = 64
HEAD_TILES = 8
HEAD_SCALAR_COLS = 192
SORT_Q_FROM = 4


def is_sorted(unit):
    return unit[0] == "k" or unit[1] >= SORT_Q_FROM


def plan():
    wq = [("q", u // 8, u % 8) for u in range(32)]
    wk = [("k", u // 4, u % 4) for u in range(16)]
    blocks = [dict(T=wq[0:1], nx=1), dict(T=wq[1:2], nx=1)]
    for g in range(8):
        blocks.append(dict(T=wq[g + 2 : g + 3], M=wq[g : g + 1], nx=(1 if g < 6 else 0)))
    for j in range(4, 16):
        blocks.append(dict(T=wq[2 * j + 2 : 2 * j + 4], M=wq[2 * j : 2 * j + 2], nx=(1 if j < 12 else 0)))
    for b in range(B):
        for n in range(NCH):
            if b == 0 and n == 0:
                continue
            for G in range(NG):
                blk = dict(T=[], S1=("q", b, n, G), nx=(2 if n < NCH - 1 else 1))
                if b == 0 and n <= 2:
                    i = 4 * (n - 1) + G
                    blk["T"] = wk[2 * i : 2 * i + 2]
                if b == 1 and n == 0:
                    blk["S2"] = (0, NCH - 1, G)
                blocks.append(blk)
        for n in range(NCH):
            for G in range(NG):
                blk = dict(T=[], S1=("k", b, n, G), nx=1)
                if n > 0:
                    blk["S2"] = (b, n - 1, G)
                if n == NCH - 1:
                    blk["nx"] = 2 if b == 0 else 0
                blocks.append(blk)
    for G in range(NG):
        blocks.append(dict(T=[], S2=(B - 1, NCH - 1, G), nx=0))
    return blocks


def tile_crossattentionvaluefuser_pa_l_kernel(tc, query_features, reference_features, Wq, bq, Wk, bk, out):
    nc = tc.nc
    feats = {
        "q": query_features.rearrange("b c h w -> b c (h w)"),
        "k": reference_features.rearrange("b c h w -> b c (h w)"),
    }
    weights = {"q": Wq, "k": Wk}
    out_rows = out.rearrange("b h w p -> b (h w) p")

    with ExitStack() as ctx:
        ctx.enter_context(tc.manual_schedule())
        const = ctx.enter_context(tc.tile_pool(name="const", bufs=1))
        keep = ctx.enter_context(tc.tile_pool(name="keep", bufs=1))
        stage = ctx.enter_context(tc.tile_pool(name="stage", bufs=2))
        psum = ctx.enter_context(tc.psum_pool(name="psum", bufs=4))

        blocks = plan()
        x_list = []
        for b in range(B):
            for s in ("q", "k"):
                for n in range(NCH):
                    for g in range(PASSES[s]):
                        x_list.append((s, b, n, g))

        load_list = []
        xi = 0
        for i, blk in enumerate(blocks):
            for unit in blk["T"]:
                if not is_sorted(unit):
                    load_list.append(("w",) + unit)
            for r in range(blk["nx"]):
                load_list.append(("x",) + x_list[xi])
                xi += 1
            if i + 1 < len(blocks):
                for unit in blocks[i + 1]["T"]:
                    if is_sorted(unit):
                        load_list.append(("w",) + unit)
        assert xi == len(x_list)
        load_pos = {}
        for i, key in enumerate(load_list):
            load_pos[key] = i
        raws = {}
        issued = [0]
        lent = [None]

        def view_of(key):
            if key[0] == "w":
                s, G, g = key[1:]
                return weights[s][KP * G : KP * (G + 1), KP * g : KP * (g + 1)].rearrange("(m t) k -> m t k", t=PACK)
            s, b, n, g = key[1:]
            return feats[s][b, KP * g : KP * (g + 1), NT * n : NT * (n + 1)].rearrange("(p j) w -> p j w", j=PACK)

        def fetch(key):
            want = min(len(load_list), max(load_pos[key], 2 * len(BORROW)) + RAW_BUFS)
            while issued[0] < want:
                i = issued[0]
                k2 = load_list[i]
                if i < 2 * len(BORROW):
                    if i % 2 == 0:
                        lent[0] = keep.tile([P, 2, PACK, NT], BF16, name=BORROW[i // 2], align_bytes=256)
                    raw = lent[0][:, i % 2]
                else:
                    raw = stage.tile([P, PACK, NT], BF16, name="raw", bufs=RAW_BUFS)
                nc.sync.dma_start(out=raw[:], in_=view_of(k2))
                raws[k2] = raw
                issued[0] += 1
            return raws[key]

        fetch(load_list[0])

        ident = const.tile([P, P], F32, name="ident")
        make_identity(nc, ident[:])
        bias = {}
        bias_raw = {}
        for s, vec in (("q", bq), ("k", bk)):
            b_raw = const.tile([P, NG, PACK], BF16, name="braw" + s)
            nc.gpsimd.dma_start(out=b_raw[:], in_=vec.rearrange("(g p t) -> p g t", g=NG, t=PACK))
            bias[s] = const.tile([P, NG * PACK], F32, name="bias" + s)
            bias_raw[s] = b_raw
        warm = const.tile([P, 1], F32, name="warm")
        nc.scalar.activation(out=warm[:], in_=ident[:, 0:1], func=IDENT, bias=0.0, scale=1.0)

        w_codes, w_planes = {}, {}
        w_plane_tile = {}

        def interleave(src, scalar_cols):
            grp = stage.tile([P, NT * PACK], BF16, name="grp", bufs=GRP_BUFS, align_bytes=64)
            dst = grp[:].rearrange("p (w j) -> p w j", j=PACK)
            cut = NT - scalar_cols
            nc.vector.tensor_copy(out=dst[:, 0:cut, :], in_=src[:, :, 0:cut].rearrange("p j w -> p w j"))
            if scalar_cols:
                nc.scalar.copy(out=dst[:, cut:NT, :], in_=src[:, :, cut:NT].rearrange("p j w -> p w j"))
            return grp

        def quantize(grp, codes, plane, slot):
            nc.vector.quantize_mx(out=codes.bitcast(FP8X4), scales=plane[4 * slot : P, :], in_=grp[:])

        def new_c8():
            codes = stage.tile([P, 4, NT], U32, name="c8", bufs=C8_BUFS, align_bytes=256)
            plane = stage.tile([P, NT + SHIFT], U8, name="c8p", bufs=C8_BUFS, align_bytes=256)
            return codes, plane[:, SHIFT : SHIFT + NT]

        sorted_words = {}

        def w_sort(unit):
            words = fetch(("w",) + unit)[:].rearrange("m t k -> m (t k)").bitcast(F32)
            srt = stage.tile([P, 2 * NT], F32, name="stg", bufs=STG_BUFS, align_bytes=64)
            nc.scalar.copy(
                out=srt[:].rearrange("m (t u p) -> m t u p", t=PACK, u=2),
                in_=words.rearrange("m (t p u) -> m t u p", t=PACK, u=2),
            )
            sorted_words[unit] = srt

        def w_transpose(units):
            banks = []
            for unit in units:
                s, G, g = unit
                if g == 0:
                    w_codes[s, G] = keep.tile([P, PASSES[s], KP], U32, name="wc%s%d" % (s, G), align_bytes=256)
                    width = PASSES[s] // 4 * KP
                    if G == 0:
                        w_plane_tile[s] = keep.tile([P, NG * width + SHIFT], U8, name="wp%s" % s, align_bytes=256)
                    w_planes[s, G] = w_plane_tile[s][:, SHIFT + G * width : SHIFT + (G + 1) * width].rearrange("p (h c) -> p h c", c=KP)
                if is_sorted(unit):
                    words = sorted_words[unit]
                else:
                    words = fetch(("w",) + unit)[:].rearrange("m t k -> m (t k)").bitcast(F32)
                for half in range(2):
                    bank = psum.tile([P, NT], F32, name="pb")
                    for tt in range(2):
                        t = 2 * half + tt
                        for u in range(2):
                            c0 = (2 * tt + u) * P
                            if is_sorted(unit):
                                src = words[:, (2 * t + u) * P : (2 * t + u + 1) * P]
                            else:
                                src = words[:, 256 * t + u : 256 * (t + 1) : 2]
                            nc.tensor.transpose(bank[:, c0 : c0 + P], src, ident[:])
                    banks.append(bank)
            return banks

        def w_evacuate(units, banks):
            tiles = []
            for i in range(len(units)):
                wg = stage.tile([P, NT * PACK], BF16, name="stg", bufs=STG_BUFS, align_bytes=64)
                wgw = wg[:].bitcast(F32)
                for half in range(2):
                    nc.scalar.copy(
                        out=wgw[:, 512 * half : 512 * (half + 1)].rearrange("p (t m u) -> p t m u", t=2, u=2),
                        in_=banks[2 * i + half][:].rearrange("p (t u m) -> p t m u", t=2, u=2),
                    )
                tiles.append(wg)
            return tiles

        def s1_matmul(acc, s, G, t, g, xc):
            codes, plane = xc[g // 4]
            nc.tensor.matmul_mx(
                out=acc[:],
                lhsT=w_codes[s, G][:, g, P * t : P * (t + 1)].bitcast(FP8X4),
                lhsT_scale=w_planes[s, G][4 * (g % 4) : P, g // 4, P * t : P * (t + 1)],
                rhs=codes[:, g % 4, :].bitcast(FP8X4),
                rhs_scale=plane[4 * (g % 4) : P, :],
                start=(g == 0),
                stop=(g == PASSES[s] - 1),
            )

        def s1_evacuate(accs, s, G):
            st = stage.tile([P, PACK, NT], BF16, name="stg", bufs=STG_BUFS, align_bytes=64)
            for t in range(PACK):
                col = PACK * G + t
                nc.scalar.activation(out=st[:, t, :], in_=accs[t][:], func=IDENT, bias=bias[s][:, col : col + 1], scale=1.0)
            return st

        def s2_part(b, n, part, q_tiles, kc, tag):
            qc, qp = q_tiles[part]
            banks4 = []
            for i4 in range(4):
                acc4 = psum.tile([P, NT], F32, name=tag)
                banks4.append(acc4)
            if b == B - 1 and n == NCH - 1 and part == 3:
                order = [(G, i4) for i4 in range(4) for G in range(NG)]
            else:
                order = [(G, i4) for G in range(NG) for i4 in range(4)]
            for G, i4 in order:
                if True:
                    c0 = i4 * P
                    nc.tensor.matmul_mx(
                        out=banks4[i4][:],
                        lhsT=qc[:, G, c0 : c0 + P].bitcast(FP8X4),
                        lhsT_scale=qp[4 * G : P, c0 : c0 + P],
                        rhs=kc[0][:, G, :].bitcast(FP8X4),
                        rhs_scale=kc[1][4 * G : P, :],
                        start=(G == 0),
                        stop=(G == NG - 1),
                    )
            for i4 in range(4):
                it = 4 * part + i4
                o = stage.tile([P, NT], F32, name="o", bufs=OUT_BUFS)
                nc.scalar.copy(out=o[:], in_=banks4[i4][:])
                nc.scalar.dma_start(out=out_rows[b, P * it : P * (it + 1), NT * n : NT * (n + 1)], in_=o[:])

        x_codes = {}
        q_tiles = {}
        k_tiles = {}
        accs = {}
        pending = []
        x_next = 0
        last_tag = ["pa"]
        late_x = {}
        w_ready = {}

        for bi, blk in enumerate(blocks):
            if bi == 4:
                for s in ("q", "k"):
                    nc.vector.tensor_copy(out=bias[s][:], in_=bias_raw[s][:].rearrange("p g t -> p (g t)"))
            units = blk["T"]
            banks = w_transpose(units)

            todo = []
            for st, codes, plane, slot in pending:
                todo.append((interleave(st, 0), codes, plane, slot))
            pending = []
            for r in range(blk["nx"]):
                s, b, n, g = x_list[x_next]
                if g % 4 == 0:
                    if g == 0:
                        x_codes[s, b, n] = []
                    x_codes[s, b, n].append(new_c8())
                codes, plane = x_codes[s, b, n][g // 4]
                raw = fetch(("x", s, b, n, g))
                if x_next < HEAD_TILES:
                    late_x[g] = (interleave(raw, HEAD_SCALAR_COLS), codes[:, g % 4, :], plane, g % 4)
                else:
                    todo.append((interleave(raw, 0), codes[:, g % 4, :], plane, g % 4))
                x_next += 1
            for grp, codes, plane, slot in todo:
                quantize(grp, codes, plane, slot)
            for unit, wg in zip(units, w_evacuate(units, banks)):
                w_ready[unit] = wg

            s1 = blk.get("S1")
            for s, G, g in blk.get("M", []):
                if g == 0:
                    for t in range(PACK):
                        accs[t] = psum.tile([P, NT], F32, name="pa")
                for t in range(PACK):
                    s1_matmul(accs[t], s, G, t, g, x_codes[s, 0, 0])
                if g == PASSES[s] - 1:
                    s1 = (s, 0, 0, G)
            if "S1" in blk:
                s, b, n, G = s1
                if units or "S2" in blk or last_tag[0] == "pb":
                    last_tag[0] = "pa"
                else:
                    last_tag[0] = "pb"
                for t in range(PACK):
                    accs[t] = psum.tile([P, NT], F32, name=last_tag[0])
                for g in range(PASSES[s]):
                    for t in range(PACK):
                        s1_matmul(accs[t], s, G, t, g, x_codes[s, b, n])

            due = [u for u in units if u[0] == "k"]
            if bi + 1 < len(blocks):
                due = due + blocks[bi + 1].get("M", [])
            for s, G, g in due:
                quantize(w_ready[s, G, g], w_codes[s, G][:, g, :], w_planes[s, G][:, g // 4, :], g % 4)
                if s == "q" and G == 0:
                    quantize(*late_x[g])

            if bi + 1 < len(blocks):
                for unit in blocks[bi + 1]["T"]:
                    if is_sorted(unit):
                        w_sort(unit)

            if s1 is not None:
                s, b, n, G = s1
                st = s1_evacuate(accs, s, G)
                if s == "q":
                    if G == 0:
                        if n == 0:
                            q_tiles[b] = []
                        qc = keep.tile([P, NG, NT], U32, name="qc%d" % n, align_bytes=256)
                        qp = keep.tile([P, NT + SHIFT], U8, name="qp%d" % n, align_bytes=256)
                        q_tiles[b].append((qc, qp[:, SHIFT : SHIFT + NT]))
                    dest = q_tiles[b][n]
                else:
                    if G == 0:
                        k_tiles[b, n] = new_c8()
                    dest = k_tiles[b, n]
                pending.append((st, dest[0][:, G, :], dest[1], G))

            if "S2" in blk:
                b, n, part = blk["S2"]
                s2_part(b, n, part, q_tiles[b], k_tiles[b, n], "pb" if ("S1" in blk or part % 2 == 1) else "pa")
